import numpy as np
import ml_dtypes


def mxq(x, axis, fmt="e4m3"):
    dtype, down = {"e4m3": (ml_dtypes.float8_e4m3fn, 7), "e5m2": (ml_dtypes.float8_e5m2, 14)}[fmt]
    v = np.moveaxis(np.asarray(x, np.float32).astype(ml_dtypes.bfloat16).astype(np.float64), axis, -1)
    blocks = v.reshape(v.shape[:-1] + (-1, 32))
    amax = np.abs(blocks).max(-1, keepdims=True)
    byte = np.maximum(np.where(amax > 0, np.frexp(amax)[1] - 1 + 127, 0) - down, 1)
    scale = np.exp2(byte - 127.0)
    codes = (blocks / scale).astype(np.float32).astype(dtype).astype(np.float64)
    return np.moveaxis((codes * scale).reshape(v.shape), -1, axis)


WIDE = False


def mx_kscale(k):
    if not WIDE:
        return np.ones(k)
    levels = np.array([10, -10, 5, -5, 0])
    a = np.random.permutation(np.resize(levels, k // 512 * 4)).reshape(k // 512, 4)
    idx = np.arange(k)
    return np.exp2(a[idx // 512, idx % 128 // 32])


BF16 = ml_dtypes.bfloat16


def bf(x):
    return np.asarray(x, np.float32).astype(BF16)


def f64(x):
    return np.asarray(x).astype(np.float64)


B, C, H, W, M, O = 2, 8192, 16, 16, 512, 512
N = B * H * W
L2_EPS = 1e-12
BN_EPS = 1e-5


def l2_normalize(x, axis):
    n = np.sqrt(np.sum(x * x, axis=axis, keepdims=True))
    return x / np.maximum(n, L2_EPS)


def setup_inputs():
    s = mx_kscale(C)
    cm = (np.random.standard_normal((N, C)) * 5.0 + np.random.standard_normal((1, C)) * 1.5) / np.sqrt(C)
    w = np.random.standard_normal((O, 2 * C)) * 0.1 / np.sqrt(2 * C)
    w[:, C:] = w[:, C:] / s
    return {"query": bf(np.random.standard_normal((B, C, H, W))), "concat_memory": bf(cm * s), "conv_w": bf(w),
            "bn_gamma": bf(1.0 + 0.1 * np.random.standard_normal(O)), "bn_beta": bf(0.2 * np.random.standard_normal(O))}


def reference(query, concat_memory, conv_w, bn_gamma, bn_beta):
    q_flat = l2_normalize(f64(query), 1).transpose(0, 2, 3, 1).reshape(N, C)
    upd = np.concatenate([q_flat, f64(concat_memory)], axis=1)
    y = mxq(upd, 1, "e4m3") @ mxq(f64(conv_w), 1, "e4m3").T
    y = y.reshape(B, H, W, O).transpose(0, 3, 1, 2)
    mean = np.mean(y, axis=(0, 2, 3), keepdims=True)
    var = np.mean((y - mean) ** 2, axis=(0, 2, 3), keepdims=True)
    y = (y - mean) / np.sqrt(var + BN_EPS)
    y = y * f64(bn_gamma)[None, :, None, None] + f64(bn_beta)[None, :, None, None]
    return np.maximum(y, 0.0)

@@ -1,0 +1,252 @@
+from contextlib import ExitStack
+
+import concourse.mybir as mybir
+from concourse.masks import make_identity
+
+F32 = mybir.dt.float32
+BF16 = mybir.dt.bfloat16
+U32 = mybir.dt.uint32
+U8 = mybir.dt.uint8
+FP8X4 = mybir.dt.float8_e4m3fn_x4
+ACT = mybir.ActivationFunctionType
+ALU = mybir.AluOpType
+AXIS = mybir.AxisListType
+
+P = 128
+BATCH = 2
+CHANNELS = 8192
+PIXELS = 256
+ROWS = BATCH * PIXELS
+OUT_CH = 512
+ROW_TILES = ROWS // P
+K_PASS = 4 * P
+K_CHUNK = 2 * K_PASS
+PASSES_PER_CHUNK = K_CHUNK // K_PASS
+HALF_CHUNKS = CHANNELS // K_CHUNK
+PLANES = CHANNELS // P
+SLAB_PLANES = 8
+SLABS = BATCH * PLANES // SLAB_PLANES
+SLABS_PER_PASS = 2
+SQUARING_CHUNKS = SLABS // (SLABS_PER_PASS * PASSES_PER_CHUNK)
+AHEAD = 3
+L2_EPS = 1e-12
+BN_EPS = 1e-5
+
+FLOPS = 2 * ROWS * OUT_CH * 2 * CHANNELS
+
+
+def tile_memory_sup_pb_k_kernel(tc, query, concat_memory, conv_w, bn_gamma, bn_beta, out):
+    nc = tc.nc
+    with ExitStack() as ctx:
+        const = ctx.enter_context(tc.tile_pool(name="const", bufs=1))
+        rows_pool = ctx.enter_context(tc.tile_pool(name="rows", bufs=AHEAD + 1))
+        work = ctx.enter_context(tc.tile_pool(name="work", bufs=3))
+        scratch = ctx.enter_context(tc.tile_pool(name="scratch", bufs=4))
+        acc_pool = ctx.enter_context(tc.psum_pool(name="acc", bufs=1))
+        bank_pool = ctx.enter_context(tc.psum_pool(name="bank", bufs=4))
+
+        gb_rows = const.tile([P, P], BF16)
+        nc.vector.memset(gb_rows[:], 0.0)
+        nc.scalar.dma_start(out=gb_rows[0:ROW_TILES, :], in_=bn_gamma.rearrange("(t p) -> t p", p=P))
+        nc.scalar.dma_start(out=gb_rows[ROW_TILES : 2 * ROW_TILES, :], in_=bn_beta.rearrange("(t p) -> t p", p=P))
+        ones = const.tile([P, P], F32)
+        nc.vector.memset(ones[:], 1.0)
+        warm = const.tile([P, 1], F32)
+        nc.scalar.sqrt(out=warm[:], in_=ones[:, 0:1])
+        ident = const.tile([P, P], F32)
+        make_identity(nc, ident[:])
+
+        q_sb = const.tile([P, BATCH, PLANES, PIXELS], BF16)
+        sum_sq = const.tile([P, BATCH, 2, PLANES // 4], F32)
+        inv_norm = const.tile([P, BATCH, PIXELS], F32)
+
+        def load_slab(slab):
+            b, first = divmod(slab * SLAB_PLANES, PLANES)
+            planes = slice(first, first + SLAB_PLANES)
+            nc.sync.dma_start(
+                out=q_sb[:, b, planes, :].rearrange("p (s e) n -> p s (e n)", e=2),
+                in_=query[b, first * P : (first + SLAB_PLANES) * P].rearrange("(s p e) h w -> p s (e h w)", p=P, e=2),
+            )
+
+        chunks = [("memory", m) for m in range(SQUARING_CHUNKS)]
+        for j in range(HALF_CHUNKS - SQUARING_CHUNKS):
+            chunks.extend([("query", 2 * j), ("query", 2 * j + 1), ("memory", SQUARING_CHUNKS + j)])
+        loaded = {}
+
+        def load_chunk(c):
+            kind, index = chunks[c]
+            cols = slice(index * K_CHUNK, (index + 1) * K_CHUNK)
+            w_first = index * K_CHUNK + (CHANNELS if kind == "memory" else 0)
+            w_cols = slice(w_first, w_first + K_CHUNK)
+            w_rows = rows_pool.tile([P, ROW_TILES, K_CHUNK], BF16, tag="w_rows")
+            nc.sync.dma_start(out=w_rows[:], in_=conv_w[:, w_cols].rearrange("(t p) k -> p t k", p=P))
+            m_rows = None
+            if kind == "memory":
+                m_rows = rows_pool.tile([P, ROW_TILES, K_CHUNK], BF16, tag="m_rows")
+                nc.sync.dma_start(out=m_rows[:], in_=concat_memory[:, cols].rearrange("(t p) k -> p t k", p=P))
+            loaded[c] = (w_rows, m_rows)
+
+        def load_step(c):
+            per_chunk = SLABS_PER_PASS * PASSES_PER_CHUNK
+            if c < SQUARING_CHUNKS:
+                for slab in range(per_chunk * c, per_chunk * c + per_chunk // 2):
+                    load_slab(slab)
+            if c < len(chunks):
+                load_chunk(c)
+            if c < SQUARING_CHUNKS:
+                for slab in range(per_chunk * c + per_chunk // 2, per_chunk * (c + 1)):
+                    load_slab(slab)
+
+        for c in range(AHEAD):
+            load_step(c)
+
+        gb_f32 = const.tile([P, P], F32)
+        nc.vector.tensor_copy(out=gb_f32[:], in_=gb_rows[:])
+        gb_bank = bank_pool.tile([P, 4, P], F32, tag="bank")
+        nc.tensor.transpose(gb_bank[:, 0, :], gb_f32[:], ident[:])
+        gamma_beta = const.tile([P, 2 * ROW_TILES], F32)
+        nc.vector.tensor_copy(out=gamma_beta[:], in_=gb_bank[:, 0, 0 : 2 * ROW_TILES])
+
+        acc = [acc_pool.tile([P, ROWS], F32, name="acc%d" % t) for t in range(ROW_TILES)]
+
+        def transpose_rows(rows, local, grouped_words, copy):
+            for pair in range(ROW_TILES // 2):
+                bank = bank_pool.tile([P, 4, P], F32, tag="bank")
+                for j in range(4):
+                    t, u = 2 * pair + j // 2, j % 2
+                    first = (2 * local + u) * P
+                    nc.tensor.transpose(bank[:, j, :], rows[:, t, :].bitcast(F32)[:, first : first + P], ident[:])
+                copy(
+                    out=grouped_words[:, 4 * P * pair : 4 * P * (pair + 1)].rearrange("p (t r u) -> p t r u", t=2, u=2),
+                    in_=bank[:].rearrange("p (t u) r -> p t r u", u=2),
+                )
+
+        def square_slab(slab):
+            b, first = divmod(slab * SLAB_PLANES, PLANES)
+            for half in range(SLAB_PLANES // 4):
+                bank = bank_pool.tile([P, 4, P], F32, tag="bank")
+                for j in range(4):
+                    plane = first + 4 * half + j
+                    nc.tensor.transpose(bank[:, j, :], q_sb[:, b, plane, :].bitcast(F32), ident[:])
+                by_parity = bank[:].bitcast(BF16).rearrange("p j (c h) -> p h j c", h=2)
+                for h in range(2):
+                    junk = scratch.tile([P, 4, P], BF16, tag="junk")
+                    k = first // 4 + half
+                    nc.scalar.activation(
+                        out=junk[:], in_=by_parity[:, h], func=ACT.Square, accum_out=sum_sq[:, b, h, k : k + 1]
+                    )
+
+        def pixel_scales(b):
+            total = scratch.tile([P, 2], F32, tag="total")
+            nc.vector.tensor_reduce(out=total[:], in_=sum_sq[:, b], axis=AXIS.X, op=ALU.add)
+            floored = scratch.tile([P, 2], F32, tag="floored")
+            nc.vector.tensor_scalar_max(out=floored[:], in0=total[:], scalar1=L2_EPS * L2_EPS)
+            norm = scratch.tile([P, 2], F32, tag="norm")
+            nc.scalar.sqrt(out=norm[:], in_=floored[:])
+            inv = scratch.tile([P, 2], F32, tag="inv")
+            nc.vector.reciprocal(out=inv[:], in_=norm[:])
+            repeated = scratch.tile([P, 2, P], F32, tag="repeated")
+            bank = bank_pool.tile([P, 4, P], F32, tag="bank")
+            for h in range(2):
+                nc.vector.tensor_scalar_mul(out=repeated[:, h, :], in0=ones[:], scalar1=inv[:, h : h + 1])
+                nc.tensor.transpose(bank[:, h, :], repeated[:, h, :], ident[:])
+            nc.vector.tensor_copy(
+                out=inv_norm[:, b, :].rearrange("p (w h) -> p w h", h=2),
+                in_=bank[:, 0:2, :].rearrange("p h w -> p w h"),
+            )
+
+        def normalise(g, grouped):
+            for b in range(BATCH):
+                first = 4 * OUT_CH + 4 * PIXELS * b
+                nc.vector.tensor_tensor(
+                    out=grouped[:, first : first + 4 * PIXELS].rearrange("p (n t) -> p n t", t=4),
+                    in0=q_sb[:, b, 4 * g : 4 * g + 4, :].rearrange("p t n -> p n t"),
+                    in1=inv_norm[:, b, :].unsqueeze(2).to_broadcast([P, PIXELS, 4]),
+                    op=ALU.mult,
+                )
+
+        passes = [(c, local) for c in range(len(chunks)) for local in range(PASSES_PER_CHUNK)]
+        grouped_of = {}
+        operands_of = {}
+
+        def prepare(i):
+            c, local = passes[i]
+            kind, index = chunks[c]
+            if local == 0:
+                load_step(c + AHEAD)
+            w_rows, m_rows = loaded[c]
+            squaring = c < SQUARING_CHUNKS
+            copy = nc.vector.tensor_copy if squaring else nc.scalar.copy
+            grouped = work.tile([P, 4 * (OUT_CH + ROWS)], BF16, tag="grouped", align_bytes=64)
+            words = grouped[:].bitcast(F32)
+            transpose_rows(w_rows, local, words[:, 0 : 2 * OUT_CH], copy)
+            if kind == "memory":
+                transpose_rows(m_rows, local, words[:, 2 * OUT_CH : 2 * (OUT_CH + ROWS)], copy)
+            else:
+                normalise(index * PASSES_PER_CHUNK + local, grouped)
+            if squaring:
+                for slab in range(SLABS_PER_PASS * i, SLABS_PER_PASS * (i + 1)):
+                    square_slab(slab)
+                    if (slab + 1) % (SLABS // BATCH) == 0:
+                        pixel_scales(slab // (SLABS // BATCH))
+            grouped_of[i] = grouped
+
+        def quantise(i):
+            codes = work.tile([P, OUT_CH + ROWS], U32, tag="codes", align_bytes=64)
+            scales = work.tile([P, OUT_CH + ROWS], U8, tag="scales", align_bytes=64)
+            nc.vector.quantize_mx(out=codes[:].bitcast(FP8X4), scales=scales[:], in_=grouped_of[i][:])
+            operands_of[i] = (codes, scales)
+
+        def multiply(i):
+            codes, scales = operands_of[i]
+            pixels = slice(OUT_CH, OUT_CH + ROWS)
+            for t in range(ROW_TILES):
+                channels = slice(t * P, (t + 1) * P)
+                nc.tensor.matmul_mx(
+                    out=acc[t][:],
+                    lhsT=codes[:, channels].bitcast(FP8X4),
+                    lhsT_scale=scales[:, channels],
+                    rhs=codes[:, pixels].bitcast(FP8X4),
+                    rhs_scale=scales[:, pixels],
+                    start=(i == 0),
+                    stop=(i == len(passes) - 1),
+                )
+
+        for i in range(len(passes) + 2):
+            if i < len(passes):
+                prepare(i)
+            if 1 <= i <= len(passes):
+                quantise(i - 1)
+            if i >= 2:
+                multiply(i - 2)
+
+        stats = const.tile([P, ROW_TILES, 6], F32)
+        mean_var = const.tile([P, ROW_TILES, 2], F32)
+        for t in range(ROW_TILES):
+            nc.vector.bn_stats(out=stats[:, t, :], in_=acc[t][:])
+            nc.vector.bn_aggr(out=mean_var[:, t, :], in_=stats[:, t, :])
+        var_eps = const.tile([P, ROW_TILES], F32)
+        nc.vector.tensor_scalar_add(out=var_eps[:], in0=mean_var[:, :, 1], scalar1=BN_EPS)
+        std = const.tile([P, ROW_TILES], F32)
+        nc.scalar.sqrt(out=std[:], in_=var_eps[:])
+        inv_std = const.tile([P, ROW_TILES], F32)
+        nc.vector.reciprocal(out=inv_std[:], in_=std[:])
+        gain = const.tile([P, ROW_TILES], F32)
+        nc.vector.tensor_tensor(out=gain[:], in0=gamma_beta[:, 0:ROW_TILES], in1=inv_std[:], op=ALU.mult)
+        mean_gain = const.tile([P, ROW_TILES], F32)
+        nc.vector.tensor_tensor(out=mean_gain[:], in0=mean_var[:, :, 0], in1=gain[:], op=ALU.mult)
+        shift = const.tile([P, ROW_TILES], F32)
+        nc.vector.tensor_tensor(
+            out=shift[:], in0=gamma_beta[:, ROW_TILES : 2 * ROW_TILES], in1=mean_gain[:], op=ALU.subtract
+        )
+        out_tiles = out.rearrange("b (t p) h w -> t p b (h w)", p=P)
+        for t in range(ROW_TILES):
+            result = scratch.tile([P, BATCH, PIXELS], F32, tag="result")
+            nc.scalar.activation(
+                out=result[:].rearrange("p b n -> p (b n)"),
+                in_=acc[t][:],
+                func=ACT.Relu,
+                scale=gain[:, t : t + 1],
+                bias=shift[:, t : t + 1],
+            )
+            nc.sync.dma_start(out=out_tiles[t], in_=result[:])

@@ -28,6 +28,8 @@ SLAB_PLANES = 8
 SLABS = BATCH * PLANES // SLAB_PLANES
 SLABS_PER_PASS = 2
 SQUARING_CHUNKS = SLABS // (SLABS_PER_PASS * PASSES_PER_CHUNK)
+BANKS_PER_PASS = SLABS_PER_PASS * SLAB_PLANES // 4
+BATCH_PASSES = PLANES // 4 // BANKS_PER_PASS
 AHEAD = 3
 L2_EPS = 1e-12
 BN_EPS = 1e-5
@@ -70,7 +72,7 @@ def tile_memory_sup_pb_k_kernel(tc, query, concat_memory, conv_w, bn_gamma, bn_b
 
         chunks = [("memory", m) for m in range(SQUARING_CHUNKS)]
         for j in range(HALF_CHUNKS - SQUARING_CHUNKS):
-            chunks.extend([("query", 2 * j), ("query", 2 * j + 1), ("memory", SQUARING_CHUNKS + j)])
+            chunks.extend([("memory", SQUARING_CHUNKS + j), ("query", 2 * j), ("query", 2 * j + 1)])
         loaded = {}
 
         def load_chunk(c):
@@ -100,43 +102,43 @@ def tile_memory_sup_pb_k_kernel(tc, query, concat_memory, conv_w, bn_gamma, bn_b
         for c in range(AHEAD):
             load_step(c)
 
-        gb_f32 = const.tile([P, P], F32)
-        nc.vector.tensor_copy(out=gb_f32[:], in_=gb_rows[:])
-        gb_bank = bank_pool.tile([P, 4, P], F32, tag="bank")
-        nc.tensor.transpose(gb_bank[:, 0, :], gb_f32[:], ident[:])
         gamma_beta = const.tile([P, 2 * ROW_TILES], F32)
-        nc.vector.tensor_copy(out=gamma_beta[:], in_=gb_bank[:, 0, 0 : 2 * ROW_TILES])
+
+        def transpose_gamma_beta():
+            gb_f32 = const.tile([P, P], F32)
+            nc.vector.tensor_copy(out=gb_f32[:], in_=gb_rows[:])
+            gb_bank = bank_pool.tile([P, 4, P], F32, tag="bank")
+            nc.tensor.transpose(gb_bank[:, 0, :], gb_f32[:], ident[:])
+            nc.vector.tensor_copy(out=gamma_beta[:], in_=gb_bank[:, 0, 0 : 2 * ROW_TILES])
 
         acc = [acc_pool.tile([P, ROWS], F32, name="acc%d" % t) for t in range(ROW_TILES)]
 
-        def transpose_rows(rows, local, grouped_words, copy):
-            for pair in range(ROW_TILES // 2):
-                bank = bank_pool.tile([P, 4, P], F32, tag="bank")
-                for j in range(4):
-                    t, u = 2 * pair + j // 2, j % 2
-                    first = (2 * local + u) * P
-                    nc.tensor.transpose(bank[:, j, :], rows[:, t, :].bitcast(F32)[:, first : first + P], ident[:])
-                copy(
-                    out=grouped_words[:, 4 * P * pair : 4 * P * (pair + 1)].rearrange("p (t r u) -> p t r u", t=2, u=2),
-                    in_=bank[:].rearrange("p (t u) r -> p t r u", u=2),
+        def transpose_rows(rows, local, pair, grouped_words, copy):
+            bank = bank_pool.tile([P, 4, P], F32, tag="bank")
+            for j in range(4):
+                t, u = 2 * pair + j // 2, j % 2
+                first = (2 * local + u) * P
+                nc.tensor.transpose(bank[:, j, :], rows[:, t, :].bitcast(F32)[:, first : first + P], ident[:])
+            copy(
+                out=grouped_words[:, 4 * P * pair : 4 * P * (pair + 1)].rearrange("p (t r u) -> p t r u", t=2, u=2),
+                in_=bank[:].rearrange("p (t u) r -> p t r u", u=2),
+            )
+
+        def square_planes(k):
+            b, first = divmod(4 * k, PLANES)
+            bank = bank_pool.tile([P, 4, P], F32, tag="bank")
+            for j in range(4):
+                nc.tensor.transpose(bank[:, j, :], q_sb[:, b, first + j, :].bitcast(F32), ident[:])
+            by_parity = bank[:].bitcast(BF16).rearrange("p j (c h) -> p h j c", h=2)
+            for h in range(2):
+                junk = scratch.tile([P, 4, P], BF16, tag="junk")
+                nc.scalar.activation(
+                    out=junk[:], in_=by_parity[:, h], func=ACT.Square, accum_out=sum_sq[:, b, h, first // 4 : first // 4 + 1]
                 )
 
-        def square_slab(slab):
-            b, first = divmod(slab * SLAB_PLANES, PLANES)
-            for half in range(SLAB_PLANES // 4):
-                bank = bank_pool.tile([P, 4, P], F32, tag="bank")
-                for j in range(4):
-                    plane = first + 4 * half + j
-                    nc.tensor.transpose(bank[:, j, :], q_sb[:, b, plane, :].bitcast(F32), ident[:])
-                by_parity = bank[:].bitcast(BF16).rearrange("p j (c h) -> p h j c", h=2)
-                for h in range(2):
-                    junk = scratch.tile([P, 4, P], BF16, tag="junk")
-                    k = first // 4 + half
-                    nc.scalar.activation(
-                        out=junk[:], in_=by_parity[:, h], func=ACT.Square, accum_out=sum_sq[:, b, h, k : k + 1]
-                    )
+        repeated_of = {}
 
-        def pixel_scales(b):
+        def pixel_scales_start(b):
             total = scratch.tile([P, 2], F32, tag="total")
             nc.vector.tensor_reduce(out=total[:], in_=sum_sq[:, b], axis=AXIS.X, op=ALU.add)
             floored = scratch.tile([P, 2], F32, tag="floored")
@@ -146,24 +148,26 @@ def tile_memory_sup_pb_k_kernel(tc, query, concat_memory, conv_w, bn_gamma, bn_b
             inv = scratch.tile([P, 2], F32, tag="inv")
             nc.vector.reciprocal(out=inv[:], in_=norm[:])
             repeated = scratch.tile([P, 2, P], F32, tag="repeated")
-            bank = bank_pool.tile([P, 4, P], F32, tag="bank")
             for h in range(2):
                 nc.vector.tensor_scalar_mul(out=repeated[:, h, :], in0=ones[:], scalar1=inv[:, h : h + 1])
-                nc.tensor.transpose(bank[:, h, :], repeated[:, h, :], ident[:])
+            repeated_of[b] = repeated
+
+        def pixel_scales_finish(b):
+            bank = bank_pool.tile([P, 4, P], F32, tag="bank")
+            for h in range(2):
+                nc.tensor.transpose(bank[:, h, :], repeated_of[b][:, h, :], ident[:])
             nc.vector.tensor_copy(
                 out=inv_norm[:, b, :].rearrange("p (w h) -> p w h", h=2),
                 in_=bank[:, 0:2, :].rearrange("p h w -> p w h"),
             )
 
         def normalise(g, grouped):
-            for b in range(BATCH):
-                first = 4 * OUT_CH + 4 * PIXELS * b
-                nc.vector.tensor_tensor(
-                    out=grouped[:, first : first + 4 * PIXELS].rearrange("p (n t) -> p n t", t=4),
-                    in0=q_sb[:, b, 4 * g : 4 * g + 4, :].rearrange("p t n -> p n t"),
-                    in1=inv_norm[:, b, :].unsqueeze(2).to_broadcast([P, PIXELS, 4]),
-                    op=ALU.mult,
-                )
+            nc.vector.tensor_tensor(
+                out=grouped[:, 4 * OUT_CH : 4 * (OUT_CH + ROWS)].rearrange("p (b n t) -> p b n t", b=BATCH, t=4),
+                in0=q_sb[:, :, 4 * g : 4 * g + 4, :].rearrange("p b t n -> p b n t"),
+                in1=inv_norm[:].unsqueeze(3).to_broadcast([P, BATCH, PIXELS, 4]),
+                op=ALU.mult,
+            )
 
         passes = [(c, local) for c in range(len(chunks)) for local in range(PASSES_PER_CHUNK)]
         grouped_of = {}
@@ -179,16 +183,24 @@ def tile_memory_sup_pb_k_kernel(tc, query, concat_memory, conv_w, bn_gamma, bn_b
             copy = nc.vector.tensor_copy if squaring else nc.scalar.copy
             grouped = work.tile([P, 4 * (OUT_CH + ROWS)], BF16, tag="grouped", align_bytes=64)
             words = grouped[:].bitcast(F32)
-            transpose_rows(w_rows, local, words[:, 0 : 2 * OUT_CH], copy)
-            if kind == "memory":
-                transpose_rows(m_rows, local, words[:, 2 * OUT_CH : 2 * (OUT_CH + ROWS)], copy)
-            else:
+            scales_due = i % BATCH_PASSES == 0 and 0 < i <= BATCH * BATCH_PASSES
+            if scales_due:
+                pixel_scales_start(i // BATCH_PASSES - 1)
+            if kind == "query":
                 normalise(index * PASSES_PER_CHUNK + local, grouped)
-            if squaring:
-                for slab in range(SLABS_PER_PASS * i, SLABS_PER_PASS * (i + 1)):
-                    square_slab(slab)
-                    if (slab + 1) % (SLABS // BATCH) == 0:
-                        pixel_scales(slab // (SLABS // BATCH))
+            for pair in range(ROW_TILES // 2):
+                transpose_rows(w_rows, local, pair, words[:, 0 : 2 * OUT_CH], copy)
+                if squaring:
+                    square_planes(BANKS_PER_PASS * i + pair)
+            if kind == "memory":
+                for pair in range(ROW_TILES // 2):
+                    transpose_rows(m_rows, local, pair, words[:, 2 * OUT_CH : 2 * (OUT_CH + ROWS)], copy)
+                    if squaring:
+                        square_planes(BANKS_PER_PASS * i + ROW_TILES // 2 + pair)
+            if scales_due:
+                pixel_scales_finish(i // BATCH_PASSES - 1)
+            if i == BATCH * BATCH_PASSES:
+                transpose_gamma_beta()
             grouped_of[i] = grouped
 
         def quantise(i):
@@ -212,13 +224,14 @@ def tile_memory_sup_pb_k_kernel(tc, query, concat_memory, conv_w, bn_gamma, bn_b
                     stop=(i == len(passes) - 1),
                 )
 
-        for i in range(len(passes) + 2):
-            if i < len(passes):
-                prepare(i)
-            if 1 <= i <= len(passes):
-                quantise(i - 1)
-            if i >= 2:
-                multiply(i - 2)
+        with tc.manual_schedule():
+            for i in range(len(passes) + 2):
+                if i < len(passes):
+                    prepare(i)
+                if 1 <= i <= len(passes):
+                    quantise(i - 1)
+                if i >= 2:
+                    multiply(i - 2)
 
         stats = const.tile([P, ROW_TILES, 6], F32)
         mean_var = const.tile([P, ROW_TILES, 2], F32)

@@ -30,6 +30,7 @@ SLABS_PER_PASS = 2
 SQUARING_CHUNKS = SLABS // (SLABS_PER_PASS * PASSES_PER_CHUNK)
 BANKS_PER_PASS = SLABS_PER_PASS * SLAB_PLANES // 4
 BATCH_PASSES = PLANES // 4 // BANKS_PER_PASS
+LAG = 2
 AHEAD = 3
 L2_EPS = 1e-12
 BN_EPS = 1e-5
@@ -191,12 +192,13 @@ def tile_memory_sup_pb_k_kernel(tc, query, concat_memory, conv_w, bn_gamma, bn_b
             for pair in range(ROW_TILES // 2):
                 transpose_rows(w_rows, local, pair, words[:, 0 : 2 * OUT_CH], copy)
                 if squaring:
-                    square_planes(BANKS_PER_PASS * i + pair)
-            if kind == "memory":
-                for pair in range(ROW_TILES // 2):
+                    square_planes(BANKS_PER_PASS * i + 2 * pair)
+                if kind == "memory":
                     transpose_rows(m_rows, local, pair, words[:, 2 * OUT_CH : 2 * (OUT_CH + ROWS)], copy)
                     if squaring:
-                        square_planes(BANKS_PER_PASS * i + ROW_TILES // 2 + pair)
+                        square_planes(BANKS_PER_PASS * i + 2 * pair + 1)
+                if i >= LAG:
+                    multiply(i - LAG, pair)
             if scales_due:
                 pixel_scales_finish(i // BATCH_PASSES - 1)
             if i == BATCH * BATCH_PASSES:
@@ -209,10 +211,10 @@ def tile_memory_sup_pb_k_kernel(tc, query, concat_memory, conv_w, bn_gamma, bn_b
             nc.vector.quantize_mx(out=codes[:].bitcast(FP8X4), scales=scales[:], in_=grouped_of[i][:])
             operands_of[i] = (codes, scales)
 
-        def multiply(i):
+        def multiply(i, pair):
             codes, scales = operands_of[i]
             pixels = slice(OUT_CH, OUT_CH + ROWS)
-            for t in range(ROW_TILES):
+            for t in range(2 * pair, 2 * pair + 2):
                 channels = slice(t * P, (t + 1) * P)
                 nc.tensor.matmul_mx(
                     out=acc[t][:],
@@ -225,13 +227,14 @@ def tile_memory_sup_pb_k_kernel(tc, query, concat_memory, conv_w, bn_gamma, bn_b
                 )
 
         with tc.manual_schedule():
-            for i in range(len(passes) + 2):
-                if i < len(passes):
-                    prepare(i)
-                if 1 <= i <= len(passes):
+            for i in range(len(passes)):
+                prepare(i)
+                if i >= 1:
                     quantise(i - 1)
-                if i >= 2:
-                    multiply(i - 2)
+            quantise(len(passes) - 1)
+            for i in range(len(passes) - LAG, len(passes)):
+                for pair in range(ROW_TILES // 2):
+                    multiply(i, pair)
 
         stats = const.tile([P, ROW_TILES, 6], F32)
         mean_var = const.tile([P, ROW_TILES, 2], F32)

@@ -18,20 +18,22 @@ CHANNELS = 8192
 PIXELS = 256
 ROWS = BATCH * PIXELS
 OUT_CH = 512
-ROW_TILES = ROWS // P
+TILES = OUT_CH // P
 K_PASS = 4 * P
-K_CHUNK = 2 * K_PASS
-PASSES_PER_CHUNK = K_CHUNK // K_PASS
-HALF_CHUNKS = CHANNELS // K_CHUNK
+HALF_PASSES = CHANNELS // K_PASS
+CHUNK_PASSES = 2
+K_CHUNK = CHUNK_PASSES * K_PASS
 PLANES = CHANNELS // P
+BANK_PLANES = 4
+BATCH_BANKS = PLANES // BANK_PLANES
 SLAB_PLANES = 8
-SLABS = BATCH * PLANES // SLAB_PLANES
-SLABS_PER_PASS = 2
-SQUARING_CHUNKS = SLABS // (SLABS_PER_PASS * PASSES_PER_CHUNK)
-BANKS_PER_PASS = SLABS_PER_PASS * SLAB_PLANES // 4
-BATCH_PASSES = PLANES // 4 // BANKS_PER_PASS
+FAST_BANKS = 4
+FAST_PASSES = BATCH_BANKS // FAST_BANKS
+SLOW_BANKS = 2
+SLOW_PASSES = BATCH_BANKS // SLOW_BANKS
+SLICES_PER_PASS = HALF_PASSES // SLOW_PASSES
+AHEAD = 2
 LAG = 2
-AHEAD = 3
 L2_EPS = 1e-12
 BN_EPS = 1e-5
 
@@ -43,15 +45,16 @@ def tile_memory_sup_pb_k_kernel(tc, query, concat_memory, conv_w, bn_gamma, bn_b
     with ExitStack() as ctx:
         const = ctx.enter_context(tc.tile_pool(name="const", bufs=1))
         rows_pool = ctx.enter_context(tc.tile_pool(name="rows", bufs=AHEAD + 1))
-        work = ctx.enter_context(tc.tile_pool(name="work", bufs=3))
+        work = ctx.enter_context(tc.tile_pool(name="work", bufs=LAG + 1))
         scratch = ctx.enter_context(tc.tile_pool(name="scratch", bufs=4))
         acc_pool = ctx.enter_context(tc.psum_pool(name="acc", bufs=1))
         bank_pool = ctx.enter_context(tc.psum_pool(name="bank", bufs=4))
 
         gb_rows = const.tile([P, P], BF16)
         nc.vector.memset(gb_rows[:], 0.0)
-        nc.scalar.dma_start(out=gb_rows[0:ROW_TILES, :], in_=bn_gamma.rearrange("(t p) -> t p", p=P))
-        nc.scalar.dma_start(out=gb_rows[ROW_TILES : 2 * ROW_TILES, :], in_=bn_beta.rearrange("(t p) -> t p", p=P))
+        nc.scalar.dma_start(out=gb_rows[0:TILES, :], in_=bn_gamma.rearrange("(t p) -> t p", p=P))
+        nc.scalar.dma_start(out=gb_rows[TILES : 2 * TILES, :], in_=bn_beta.rearrange("(t p) -> t p", p=P))
+        gamma_beta = const.tile([P, 2 * TILES], F32)
         ones = const.tile([P, P], F32)
         nc.vector.memset(ones[:], 1.0)
         warm = const.tile([P, 1], F32)
@@ -60,59 +63,56 @@ def tile_memory_sup_pb_k_kernel(tc, query, concat_memory, conv_w, bn_gamma, bn_b
         make_identity(nc, ident[:])
 
         q_sb = const.tile([P, BATCH, PLANES, PIXELS], BF16)
-        sum_sq = const.tile([P, BATCH, 2, PLANES // 4], F32)
+        sum_sq = const.tile([P, BATCH, 2, BATCH_BANKS], F32)
         inv_norm = const.tile([P, BATCH, PIXELS], F32)
+        q_codes = const.tile([P, HALF_PASSES, ROWS], U32, align_bytes=64)
+        q_scales = const.tile([P, HALF_PASSES, ROWS], U8, align_bytes=64)
+        acc = [acc_pool.tile([P, ROWS], F32, name="acc%d" % t) for t in range(TILES)]
 
         def load_slab(slab):
             b, first = divmod(slab * SLAB_PLANES, PLANES)
-            planes = slice(first, first + SLAB_PLANES)
             nc.sync.dma_start(
-                out=q_sb[:, b, planes, :].rearrange("p (s e) n -> p s (e n)", e=2),
+                out=q_sb[:, b, first : first + SLAB_PLANES, :].rearrange("p (s e) n -> p s (e n)", e=2),
                 in_=query[b, first * P : (first + SLAB_PLANES) * P].rearrange("(s p e) h w -> p s (e h w)", p=P, e=2),
             )
 
-        chunks = [("memory", m) for m in range(SQUARING_CHUNKS)]
-        for j in range(HALF_CHUNKS - SQUARING_CHUNKS):
-            chunks.extend([("memory", SQUARING_CHUNKS + j), ("query", 2 * j), ("query", 2 * j + 1)])
-        loaded = {}
+        passes = [("memory", g) for g in range(HALF_PASSES)] + [("query", g) for g in range(HALF_PASSES)]
+        chunk_rows = {}
 
         def load_chunk(c):
-            kind, index = chunks[c]
-            cols = slice(index * K_CHUNK, (index + 1) * K_CHUNK)
-            w_first = index * K_CHUNK + (CHANNELS if kind == "memory" else 0)
-            w_cols = slice(w_first, w_first + K_CHUNK)
-            w_rows = rows_pool.tile([P, ROW_TILES, K_CHUNK], BF16, tag="w_rows")
-            nc.sync.dma_start(out=w_rows[:], in_=conv_w[:, w_cols].rearrange("(t p) k -> p t k", p=P))
+            kind, g = passes[c * CHUNK_PASSES]
+            first = g * K_PASS
+            w_first = first + (CHANNELS if kind == "memory" else 0)
+            w_rows = rows_pool.tile([P, TILES, K_CHUNK], BF16, tag="w_rows")
+            nc.sync.dma_start(
+                out=w_rows[:], in_=conv_w[:, w_first : w_first + K_CHUNK].rearrange("(t p) k -> p t k", p=P)
+            )
             m_rows = None
             if kind == "memory":
-                m_rows = rows_pool.tile([P, ROW_TILES, K_CHUNK], BF16, tag="m_rows")
-                nc.sync.dma_start(out=m_rows[:], in_=concat_memory[:, cols].rearrange("(t p) k -> p t k", p=P))
-            loaded[c] = (w_rows, m_rows)
+                m_rows = rows_pool.tile([P, TILES, K_CHUNK], BF16, tag="m_rows")
+                nc.sync.dma_start(
+                    out=m_rows[:], in_=concat_memory[:, first : first + K_CHUNK].rearrange("(t p) k -> p t k", p=P)
+                )
+            chunk_rows[c] = (w_rows, m_rows)
 
-        def load_step(c):
-            per_chunk = SLABS_PER_PASS * PASSES_PER_CHUNK
-            if c < SQUARING_CHUNKS:
-                for slab in range(per_chunk * c, per_chunk * c + per_chunk // 2):
-                    load_slab(slab)
-            if c < len(chunks):
-                load_chunk(c)
-            if c < SQUARING_CHUNKS:
-                for slab in range(per_chunk * c + per_chunk // 2, per_chunk * (c + 1)):
-                    load_slab(slab)
+        def banks_squared(i):
+            if i < FAST_PASSES:
+                return range(FAST_BANKS * i, FAST_BANKS * (i + 1))
+            if i < FAST_PASSES + SLOW_PASSES:
+                first = BATCH_BANKS + SLOW_BANKS * (i - FAST_PASSES)
+                return range(first, first + SLOW_BANKS)
+            return range(0)
 
-        for c in range(AHEAD):
-            load_step(c)
-
-        gamma_beta = const.tile([P, 2 * ROW_TILES], F32)
-
-        def transpose_gamma_beta():
-            gb_f32 = const.tile([P, P], F32)
-            nc.vector.tensor_copy(out=gb_f32[:], in_=gb_rows[:])
-            gb_bank = bank_pool.tile([P, 4, P], F32, tag="bank")
-            nc.tensor.transpose(gb_bank[:, 0, :], gb_f32[:], ident[:])
-            nc.vector.tensor_copy(out=gamma_beta[:], in_=gb_bank[:, 0, 0 : 2 * ROW_TILES])
-
-        acc = [acc_pool.tile([P, ROWS], F32, name="acc%d" % t) for t in range(ROW_TILES)]
+        def load_for_chunk(c):
+            if c * CHUNK_PASSES >= len(passes):
+                return
+            banks = [k for i in range(c * CHUNK_PASSES, (c + 1) * CHUNK_PASSES) for k in banks_squared(i)]
+            slabs = sorted(set(k * BANK_PLANES // SLAB_PLANES for k in banks))
+            for slab in slabs[:1]:
+                load_slab(slab)
+            load_chunk(c)
+            for slab in slabs[1:]:
+                load_slab(slab)
 
         def transpose_rows(rows, local, pair, grouped_words, copy):
             bank = bank_pool.tile([P, 4, P], F32, tag="bank")
@@ -125,16 +125,19 @@ def tile_memory_sup_pb_k_kernel(tc, query, concat_memory, conv_w, bn_gamma, bn_b
                 in_=bank[:].rearrange("p (t u) r -> p t r u", u=2),
             )
 
-        def square_planes(k):
-            b, first = divmod(4 * k, PLANES)
+        def square_bank(k):
+            b, first = divmod(k * BANK_PLANES, PLANES)
             bank = bank_pool.tile([P, 4, P], F32, tag="bank")
-            for j in range(4):
+            for j in range(BANK_PLANES):
                 nc.tensor.transpose(bank[:, j, :], q_sb[:, b, first + j, :].bitcast(F32), ident[:])
             by_parity = bank[:].bitcast(BF16).rearrange("p j (c h) -> p h j c", h=2)
             for h in range(2):
-                junk = scratch.tile([P, 4, P], BF16, tag="junk")
+                squares = scratch.tile([P, 4, P], BF16, tag="squares")
                 nc.scalar.activation(
-                    out=junk[:], in_=by_parity[:, h], func=ACT.Square, accum_out=sum_sq[:, b, h, first // 4 : first // 4 + 1]
+                    out=squares[:],
+                    in_=by_parity[:, h],
+                    func=ACT.Square,
+                    accum_out=sum_sq[:, b, h, k % BATCH_BANKS : k % BATCH_BANKS + 1],
                 )
 
         repeated_of = {}
@@ -162,101 +165,125 @@ def tile_memory_sup_pb_k_kernel(tc, query, concat_memory, conv_w, bn_gamma, bn_b
                 in_=bank[:, 0:2, :].rearrange("p h w -> p w h"),
             )
 
-        def normalise(g, grouped):
+        def transpose_gamma_beta():
+            gb_f32 = const.tile([P, P], F32)
+            nc.vector.tensor_copy(out=gb_f32[:], in_=gb_rows[:])
+            bank = bank_pool.tile([P, 4, P], F32, tag="bank")
+            nc.tensor.transpose(bank[:, 0, :], gb_f32[:], ident[:])
+            nc.vector.tensor_copy(out=gamma_beta[:], in_=bank[:, 0, 0 : 2 * TILES])
+
+        def normalise(b, first, count):
+            q_flat = work.tile([P, count, PIXELS, 4], BF16, tag="q_flat", align_bytes=64)
             nc.vector.tensor_tensor(
-                out=grouped[:, 4 * OUT_CH : 4 * (OUT_CH + ROWS)].rearrange("p (b n t) -> p b n t", b=BATCH, t=4),
-                in0=q_sb[:, :, 4 * g : 4 * g + 4, :].rearrange("p b t n -> p b n t"),
-                in1=inv_norm[:].unsqueeze(3).to_broadcast([P, BATCH, PIXELS, 4]),
+                out=q_flat[:],
+                in0=q_sb[:, b, 4 * first : 4 * (first + count), :].rearrange("p (g t) n -> p g n t", t=4),
+                in1=inv_norm[:, b, :].unsqueeze(1).unsqueeze(3).to_broadcast([P, count, PIXELS, 4]),
                 op=ALU.mult,
             )
+            return [(b, first + k, q_flat[:, k].rearrange("p n t -> p (n t)")) for k in range(count)]
 
-        passes = [(c, local) for c in range(len(chunks)) for local in range(PASSES_PER_CHUNK)]
+        def quantise_slices(slices):
+            for b, g, q_flat in slices:
+                pixels = slice(b * PIXELS, (b + 1) * PIXELS)
+                nc.vector.quantize_mx(out=q_codes[:, g, pixels].bitcast(FP8X4), scales=q_scales[:, g, pixels], in_=q_flat)
+
         grouped_of = {}
         operands_of = {}
 
         def prepare(i):
-            c, local = passes[i]
-            kind, index = chunks[c]
+            kind, g = passes[i]
+            c, local = divmod(i, CHUNK_PASSES)
             if local == 0:
-                load_step(c + AHEAD)
-            w_rows, m_rows = loaded[c]
-            squaring = c < SQUARING_CHUNKS
-            copy = nc.vector.tensor_copy if squaring else nc.scalar.copy
+                load_for_chunk(c + AHEAD)
+            w_rows, m_rows = chunk_rows[c]
+            copy = nc.vector.tensor_copy if i < FAST_PASSES else nc.scalar.copy
             grouped = work.tile([P, 4 * (OUT_CH + ROWS)], BF16, tag="grouped", align_bytes=64)
             words = grouped[:].bitcast(F32)
-            scales_due = i % BATCH_PASSES == 0 and 0 < i <= BATCH * BATCH_PASSES
-            if scales_due:
-                pixel_scales_start(i // BATCH_PASSES - 1)
-            if kind == "query":
-                normalise(index * PASSES_PER_CHUNK + local, grouped)
-            for pair in range(ROW_TILES // 2):
-                transpose_rows(w_rows, local, pair, words[:, 0 : 2 * OUT_CH], copy)
-                if squaring:
-                    square_planes(BANKS_PER_PASS * i + 2 * pair)
-                if kind == "memory":
-                    transpose_rows(m_rows, local, pair, words[:, 2 * OUT_CH : 2 * (OUT_CH + ROWS)], copy)
-                    if squaring:
-                        square_planes(BANKS_PER_PASS * i + 2 * pair + 1)
-                if i >= LAG:
-                    multiply(i - LAG, pair)
-            if scales_due:
-                pixel_scales_finish(i // BATCH_PASSES - 1)
-            if i == BATCH * BATCH_PASSES:
+            to_copy = [(w_rows, pair, words[:, 0 : 2 * OUT_CH]) for pair in range(TILES // 2)]
+            if kind == "memory":
+                to_copy.extend([(m_rows, pair, words[:, 2 * OUT_CH : 2 * (OUT_CH + ROWS)]) for pair in range(TILES // 2)])
+            to_square = list(banks_squared(i))
+            due = [b for b in range(BATCH) if i == (FAST_PASSES, FAST_PASSES + SLOW_PASSES)[b]]
+            for b in due:
+                pixel_scales_start(b)
+            for k in range(len(to_copy)):
+                if k < len(to_square):
+                    square_bank(to_square[k])
+                rows, pair, half = to_copy[k]
+                transpose_rows(rows, local, pair, half, copy)
+            for b in due:
+                pixel_scales_finish(b)
+            if i == FAST_PASSES + SLOW_PASSES:
                 transpose_gamma_beta()
             grouped_of[i] = grouped
+            if FAST_PASSES <= i < FAST_PASSES + SLOW_PASSES:
+                return normalise(0, SLICES_PER_PASS * (i - FAST_PASSES), SLICES_PER_PASS)
+            if kind == "query":
+                return normalise(1, g, 1)
+            return []
 
         def quantise(i):
+            width = OUT_CH + (ROWS if passes[i][0] == "memory" else 0)
             codes = work.tile([P, OUT_CH + ROWS], U32, tag="codes", align_bytes=64)
             scales = work.tile([P, OUT_CH + ROWS], U8, tag="scales", align_bytes=64)
-            nc.vector.quantize_mx(out=codes[:].bitcast(FP8X4), scales=scales[:], in_=grouped_of[i][:])
+            nc.vector.quantize_mx(
+                out=codes[:, 0:width].bitcast(FP8X4), scales=scales[:, 0:width], in_=grouped_of[i][:, 0 : 4 * width]
+            )
             operands_of[i] = (codes, scales)
 
-        def multiply(i, pair):
+        def multiply(i, t):
+            kind, g = passes[i]
             codes, scales = operands_of[i]
-            pixels = slice(OUT_CH, OUT_CH + ROWS)
-            for t in range(2 * pair, 2 * pair + 2):
-                channels = slice(t * P, (t + 1) * P)
-                nc.tensor.matmul_mx(
-                    out=acc[t][:],
-                    lhsT=codes[:, channels].bitcast(FP8X4),
-                    lhsT_scale=scales[:, channels],
-                    rhs=codes[:, pixels].bitcast(FP8X4),
-                    rhs_scale=scales[:, pixels],
-                    start=(i == 0),
-                    stop=(i == len(passes) - 1),
-                )
+            if kind == "memory":
+                upd_codes, upd_scales = codes[:, OUT_CH : OUT_CH + ROWS], scales[:, OUT_CH : OUT_CH + ROWS]
+            else:
+                upd_codes, upd_scales = q_codes[:, g, :], q_scales[:, g, :]
+            nc.tensor.matmul_mx(
+                out=acc[t][:],
+                lhsT=codes[:, t * P : (t + 1) * P].bitcast(FP8X4),
+                lhsT_scale=scales[:, t * P : (t + 1) * P],
+                rhs=upd_codes.bitcast(FP8X4),
+                rhs_scale=upd_scales,
+                start=(i == 0),
+                stop=(i == len(passes) - 1),
+            )
+
+        for c in range(AHEAD):
+            load_for_chunk(c)
 
         with tc.manual_schedule():
             for i in range(len(passes)):
-                prepare(i)
+                slices = prepare(i)
                 if i >= 1:
                     quantise(i - 1)
+                quantise_slices(slices)
+                if i >= LAG:
+                    for t in range(TILES):
+                        multiply(i - LAG, t)
             quantise(len(passes) - 1)
-            for i in range(len(passes) - LAG, len(passes)):
-                for pair in range(ROW_TILES // 2):
-                    multiply(i, pair)
+            for t in range(TILES):
+                for i in range(len(passes) - LAG, len(passes)):
+                    multiply(i, t)
 
-        stats = const.tile([P, ROW_TILES, 6], F32)
-        mean_var = const.tile([P, ROW_TILES, 2], F32)
-        for t in range(ROW_TILES):
+        stats = const.tile([P, TILES, 6], F32)
+        mean_var = const.tile([P, TILES, 2], F32)
+        for t in range(TILES):
             nc.vector.bn_stats(out=stats[:, t, :], in_=acc[t][:])
             nc.vector.bn_aggr(out=mean_var[:, t, :], in_=stats[:, t, :])
-        var_eps = const.tile([P, ROW_TILES], F32)
+        var_eps = const.tile([P, TILES], F32)
         nc.vector.tensor_scalar_add(out=var_eps[:], in0=mean_var[:, :, 1], scalar1=BN_EPS)
-        std = const.tile([P, ROW_TILES], F32)
+        std = const.tile([P, TILES], F32)
         nc.scalar.sqrt(out=std[:], in_=var_eps[:])
-        inv_std = const.tile([P, ROW_TILES], F32)
+        inv_std = const.tile([P, TILES], F32)
         nc.vector.reciprocal(out=inv_std[:], in_=std[:])
-        gain = const.tile([P, ROW_TILES], F32)
-        nc.vector.tensor_tensor(out=gain[:], in0=gamma_beta[:, 0:ROW_TILES], in1=inv_std[:], op=ALU.mult)
-        mean_gain = const.tile([P, ROW_TILES], F32)
+        gain = const.tile([P, TILES], F32)
+        nc.vector.tensor_tensor(out=gain[:], in0=gamma_beta[:, 0:TILES], in1=inv_std[:], op=ALU.mult)
+        mean_gain = const.tile([P, TILES], F32)
         nc.vector.tensor_tensor(out=mean_gain[:], in0=mean_var[:, :, 0], in1=gain[:], op=ALU.mult)
-        shift = const.tile([P, ROW_TILES], F32)
-        nc.vector.tensor_tensor(
-            out=shift[:], in0=gamma_beta[:, ROW_TILES : 2 * ROW_TILES], in1=mean_gain[:], op=ALU.subtract
-        )
+        shift = const.tile([P, TILES], F32)
+        nc.vector.tensor_tensor(out=shift[:], in0=gamma_beta[:, TILES : 2 * TILES], in1=mean_gain[:], op=ALU.subtract)
         out_tiles = out.rearrange("b (t p) h w -> t p b (h w)", p=P)
-        for t in range(ROW_TILES):
+        for t in range(TILES):
             result = scratch.tile([P, BATCH, PIXELS], F32, tag="result")
             nc.scalar.activation(
                 out=result[:].rearrange("p b n -> p (b n)"),

@@ -32,6 +32,7 @@ FAST_PASSES = BATCH_BANKS // FAST_BANKS
 SLOW_BANKS = 2
 SLOW_PASSES = BATCH_BANKS // SLOW_BANKS
 SLICES_PER_PASS = HALF_PASSES // SLOW_PASSES
+RUN = 4
 AHEAD = 2
 LAG = 2
 L2_EPS = 1e-12
@@ -174,12 +175,17 @@ def tile_memory_sup_pb_k_kernel(tc, query, concat_memory, conv_w, bn_gamma, bn_b
 
         def normalise(b, first, count):
             q_flat = work.tile([P, count, PIXELS, 4], BF16, tag="q_flat", align_bytes=64)
-            nc.vector.tensor_tensor(
-                out=q_flat[:],
-                in0=q_sb[:, b, 4 * first : 4 * (first + count), :].rearrange("p (g t) n -> p g n t", t=4),
-                in1=inv_norm[:, b, :].unsqueeze(1).unsqueeze(3).to_broadcast([P, count, PIXELS, 4]),
-                op=ALU.mult,
-            )
+            for k in range(count):
+                g = first + k
+                nc.vector.tensor_tensor(
+                    out=q_flat[:, k].rearrange("p (c i) t -> p c t i", i=RUN),
+                    in0=q_sb[:, b, 4 * g : 4 * g + 4, :].rearrange("p t (c i) -> p c t i", i=RUN),
+                    in1=inv_norm[:, b, :]
+                    .rearrange("p (c i) -> p c i", i=RUN)
+                    .unsqueeze(2)
+                    .to_broadcast([P, PIXELS // RUN, 4, RUN]),
+                    op=ALU.mult,
+                )
             return [(b, first + k, q_flat[:, k].rearrange("p n t -> p (n t)")) for k in range(count)]
 
         def quantise_slices(slices):

@@ -257,19 +257,18 @@ def tile_memory_sup_pb_k_kernel(tc, query, concat_memory, conv_w, bn_gamma, bn_b
         for c in range(AHEAD):
             load_for_chunk(c)
 
-        with tc.manual_schedule():
-            for i in range(len(passes)):
-                slices = prepare(i)
-                if i >= 1:
-                    quantise(i - 1)
-                quantise_slices(slices)
-                if i >= LAG:
-                    for t in range(TILES):
-                        multiply(i - LAG, t)
-            quantise(len(passes) - 1)
-            for t in range(TILES):
-                for i in range(len(passes) - LAG, len(passes)):
-                    multiply(i, t)
+        for i in range(len(passes)):
+            slices = prepare(i)
+            if i >= 1:
+                quantise(i - 1)
+            quantise_slices(slices)
+            if i >= LAG:
+                for t in range(TILES):
+                    multiply(i - LAG, t)
+        quantise(len(passes) - 1)
+        for t in range(TILES):
+            for i in range(len(passes) - LAG, len(passes)):
+                multiply(i, t)
 
         stats = const.tile([P, TILES, 6], F32)
         mean_var = const.tile([P, TILES, 2], F32)

from contextlib import ExitStack

import concourse.mybir as mybir
from concourse.masks import make_identity

F32 = mybir.dt.float32
BF16 = mybir.dt.bfloat16
U32 = mybir.dt.uint32
U8 = mybir.dt.uint8
FP8X4 = mybir.dt.float8_e4m3fn_x4
ACT = mybir.ActivationFunctionType
ALU = mybir.AluOpType
AXIS = mybir.AxisListType

P = 128
BATCH = 2
CHANNELS = 8192
PIXELS = 256
ROWS = BATCH * PIXELS
OUT_CH = 512
TILES = OUT_CH // P
K_PASS = 4 * P
HALF_PASSES = CHANNELS // K_PASS
CHUNK_PASSES = 2
K_CHUNK = CHUNK_PASSES * K_PASS
PLANES = CHANNELS // P
BANK_PLANES = 4
BATCH_BANKS = PLANES // BANK_PLANES
SLAB_PLANES = 8
FAST_BANKS = 4
FAST_PASSES = BATCH_BANKS // FAST_BANKS
SLOW_BANKS = 2
SLOW_PASSES = BATCH_BANKS // SLOW_BANKS
SLICES_PER_PASS = HALF_PASSES // SLOW_PASSES
RUN = 4
AHEAD = 2
LAG = 2
L2_EPS = 1e-12
BN_EPS = 1e-5

FLOPS = 2 * ROWS * OUT_CH * 2 * CHANNELS


def tile_memory_sup_pb_k_kernel(tc, query, concat_memory, conv_w, bn_gamma, bn_beta, out):
    nc = tc.nc
    with ExitStack() as ctx:
        const = ctx.enter_context(tc.tile_pool(name="const", bufs=1))
        rows_pool = ctx.enter_context(tc.tile_pool(name="rows", bufs=AHEAD + 1))
        work = ctx.enter_context(tc.tile_pool(name="work", bufs=LAG + 1))
        scratch = ctx.enter_context(tc.tile_pool(name="scratch", bufs=4))
        acc_pool = ctx.enter_context(tc.psum_pool(name="acc", bufs=1))
        bank_pool = ctx.enter_context(tc.psum_pool(name="bank", bufs=4))

        gb_rows = const.tile([P, P], BF16)
        nc.vector.memset(gb_rows[:], 0.0)
        nc.scalar.dma_start(out=gb_rows[0:TILES, :], in_=bn_gamma.rearrange("(t p) -> t p", p=P))
        nc.scalar.dma_start(out=gb_rows[TILES : 2 * TILES, :], in_=bn_beta.rearrange("(t p) -> t p", p=P))
        gamma_beta = const.tile([P, 2 * TILES], F32)
        ones = const.tile([P, P], F32)
        nc.vector.memset(ones[:], 1.0)
        warm = const.tile([P, 1], F32)
        nc.scalar.sqrt(out=warm[:], in_=ones[:, 0:1])
        ident = const.tile([P, P], F32)
        make_identity(nc, ident[:])

        q_sb = const.tile([P, BATCH, PLANES, PIXELS], BF16)
        sum_sq = const.tile([P, BATCH, 2, BATCH_BANKS], F32)
        inv_norm = const.tile([P, BATCH, PIXELS], F32)
        q_codes = const.tile([P, HALF_PASSES, ROWS], U32, align_bytes=64)
        q_scales = const.tile([P, HALF_PASSES, ROWS], U8, align_bytes=64)
        acc = [acc_pool.tile([P, ROWS], F32, name="acc%d" % t) for t in range(TILES)]

        def load_slab(slab):
            b, first = divmod(slab * SLAB_PLANES, PLANES)
            nc.sync.dma_start(
                out=q_sb[:, b, first : first + SLAB_PLANES, :].rearrange("p (s e) n -> p s (e n)", e=2),
                in_=query[b, first * P : (first + SLAB_PLANES) * P].rearrange("(s p e) h w -> p s (e h w)", p=P, e=2),
            )

        passes = [("memory", g) for g in range(HALF_PASSES)] + [("query", g) for g in range(HALF_PASSES)]
        chunk_rows = {}

        def load_chunk(c):
            kind, g = passes[c * CHUNK_PASSES]
            first = g * K_PASS
            w_first = first + (CHANNELS if kind == "memory" else 0)
            w_rows = rows_pool.tile([P, TILES, K_CHUNK], BF16, tag="w_rows")
            nc.sync.dma_start(
                out=w_rows[:], in_=conv_w[:, w_first : w_first + K_CHUNK].rearrange("(t p) k -> p t k", p=P)
            )
            m_rows = None
            if kind == "memory":
                m_rows = rows_pool.tile([P, TILES, K_CHUNK], BF16, tag="m_rows")
                nc.sync.dma_start(
                    out=m_rows[:], in_=concat_memory[:, first : first + K_CHUNK].rearrange("(t p) k -> p t k", p=P)
                )
            chunk_rows[c] = (w_rows, m_rows)

        def banks_squared(i):
            if i < FAST_PASSES:
                return range(FAST_BANKS * i, FAST_BANKS * (i + 1))
            if i < FAST_PASSES + SLOW_PASSES:
                first = BATCH_BANKS + SLOW_BANKS * (i - FAST_PASSES)
                return range(first, first + SLOW_BANKS)
            return range(0)

        def load_for_chunk(c):
            if c * CHUNK_PASSES >= len(passes):
                return
            banks = [k for i in range(c * CHUNK_PASSES, (c + 1) * CHUNK_PASSES) for k in banks_squared(i)]
            slabs = sorted(set(k * BANK_PLANES // SLAB_PLANES for k in banks))
            for slab in slabs[:1]:
                load_slab(slab)
            load_chunk(c)
            for slab in slabs[1:]:
                load_slab(slab)

        def transpose_rows(rows, local, pair, grouped_words, copy):
            bank = bank_pool.tile([P, 4, P], F32, tag="bank")
            for j in range(4):
                t, u = 2 * pair + j // 2, j % 2
                first = (2 * local + u) * P
                nc.tensor.transpose(bank[:, j, :], rows[:, t, :].bitcast(F32)[:, first : first + P], ident[:])
            copy(
                out=grouped_words[:, 4 * P * pair : 4 * P * (pair + 1)].rearrange("p (t r u) -> p t r u", t=2, u=2),
                in_=bank[:].rearrange("p (t u) r -> p t r u", u=2),
            )

        def square_bank(k):
            b, first = divmod(k * BANK_PLANES, PLANES)
            bank = bank_pool.tile([P, 4, P], F32, tag="bank")
            for j in range(BANK_PLANES):
                nc.tensor.transpose(bank[:, j, :], q_sb[:, b, first + j, :].bitcast(F32), ident[:])
            by_parity = bank[:].bitcast(BF16).rearrange("p j (c h) -> p h j c", h=2)
            for h in range(2):
                squares = scratch.tile([P, 4, P], BF16, tag="squares")
                nc.scalar.activation(
                    out=squares[:],
                    in_=by_parity[:, h],
                    func=ACT.Square,
                    accum_out=sum_sq[:, b, h, k % BATCH_BANKS : k % BATCH_BANKS + 1],
                )

        repeated_of = {}

        def pixel_scales_start(b):
            total = scratch.tile([P, 2], F32, tag="total")
            nc.vector.tensor_reduce(out=total[:], in_=sum_sq[:, b], axis=AXIS.X, op=ALU.add)
            floored = scratch.tile([P, 2], F32, tag="floored")
            nc.vector.tensor_scalar_max(out=floored[:], in0=total[:], scalar1=L2_EPS * L2_EPS)
            norm = scratch.tile([P, 2], F32, tag="norm")
            nc.scalar.sqrt(out=norm[:], in_=floored[:])
            inv = scratch.tile([P, 2], F32, tag="inv")
            nc.vector.reciprocal(out=inv[:], in_=norm[:])
            repeated = scratch.tile([P, 2, P], F32, tag="repeated")
            for h in range(2):
                nc.vector.tensor_scalar_mul(out=repeated[:, h, :], in0=ones[:], scalar1=inv[:, h : h + 1])
            repeated_of[b] = repeated

        def pixel_scales_finish(b):
            bank = bank_pool.tile([P, 4, P], F32, tag="bank")
            for h in range(2):
                nc.tensor.transpose(bank[:, h, :], repeated_of[b][:, h, :], ident[:])
            nc.vector.tensor_copy(
                out=inv_norm[:, b, :].rearrange("p (w h) -> p w h", h=2),
                in_=bank[:, 0:2, :].rearrange("p h w -> p w h"),
            )

        def transpose_gamma_beta():
            gb_f32 = const.tile([P, P], F32)
            nc.vector.tensor_copy(out=gb_f32[:], in_=gb_rows[:])
            bank = bank_pool.tile([P, 4, P], F32, tag="bank")
            nc.tensor.transpose(bank[:, 0, :], gb_f32[:], ident[:])
            nc.vector.tensor_copy(out=gamma_beta[:], in_=bank[:, 0, 0 : 2 * TILES])

        def normalise(b, first, count):
            q_flat = work.tile([P, count, PIXELS, 4], BF16, tag="q_flat", align_bytes=64)
            for k in range(count):
                g = first + k
                nc.vector.tensor_tensor(
                    out=q_flat[:, k].rearrange("p (c i) t -> p c t i", i=RUN),
                    in0=q_sb[:, b, 4 * g : 4 * g + 4, :].rearrange("p t (c i) -> p c t i", i=RUN),
                    in1=inv_norm[:, b, :]
                    .rearrange("p (c i) -> p c i", i=RUN)
                    .unsqueeze(2)
                    .to_broadcast([P, PIXELS // RUN, 4, RUN]),
                    op=ALU.mult,
                )
            return [(b, first + k, q_flat[:, k].rearrange("p n t -> p (n t)")) for k in range(count)]

        def quantise_slices(slices):
            for b, g, q_flat in slices:
                pixels = slice(b * PIXELS, (b + 1) * PIXELS)
                nc.vector.quantize_mx(out=q_codes[:, g, pixels].bitcast(FP8X4), scales=q_scales[:, g, pixels], in_=q_flat)

        grouped_of = {}
        operands_of = {}

        def prepare(i):
            kind, g = passes[i]
            c, local = divmod(i, CHUNK_PASSES)
            if local == 0:
                load_for_chunk(c + AHEAD)
            w_rows, m_rows = chunk_rows[c]
            copy = nc.vector.tensor_copy if i < FAST_PASSES else nc.scalar.copy
            grouped = work.tile([P, 4 * (OUT_CH + ROWS)], BF16, tag="grouped", align_bytes=64)
            words = grouped[:].bitcast(F32)
            to_copy = [(w_rows, pair, words[:, 0 : 2 * OUT_CH]) for pair in range(TILES // 2)]
            if kind == "memory":
                to_copy.extend([(m_rows, pair, words[:, 2 * OUT_CH : 2 * (OUT_CH + ROWS)]) for pair in range(TILES // 2)])
            to_square = list(banks_squared(i))
            due = [b for b in range(BATCH) if i == (FAST_PASSES, FAST_PASSES + SLOW_PASSES)[b]]
            for b in due:
                pixel_scales_start(b)
            for k in range(len(to_copy)):
                if k < len(to_square):
                    square_bank(to_square[k])
                rows, pair, half = to_copy[k]
                transpose_rows(rows, local, pair, half, copy)
            for b in due:
                pixel_scales_finish(b)
            if i == FAST_PASSES + SLOW_PASSES:
                transpose_gamma_beta()
            grouped_of[i] = grouped
            if FAST_PASSES <= i < FAST_PASSES + SLOW_PASSES:
                return normalise(0, SLICES_PER_PASS * (i - FAST_PASSES), SLICES_PER_PASS)
            if kind == "query":
                return normalise(1, g, 1)
            return []

        def quantise(i):
            width = OUT_CH + (ROWS if passes[i][0] == "memory" else 0)
            codes = work.tile([P, OUT_CH + ROWS], U32, tag="codes", align_bytes=64)
            scales = work.tile([P, OUT_CH + ROWS], U8, tag="scales", align_bytes=64)
            nc.vector.quantize_mx(
                out=codes[:, 0:width].bitcast(FP8X4), scales=scales[:, 0:width], in_=grouped_of[i][:, 0 : 4 * width]
            )
            operands_of[i] = (codes, scales)

        def multiply(i, t):
            kind, g = passes[i]
            codes, scales = operands_of[i]
            if kind == "memory":
                upd_codes, upd_scales = codes[:, OUT_CH : OUT_CH + ROWS], scales[:, OUT_CH : OUT_CH + ROWS]
            else:
                upd_codes, upd_scales = q_codes[:, g, :], q_scales[:, g, :]
            nc.tensor.matmul_mx(
                out=acc[t][:],
                lhsT=codes[:, t * P : (t + 1) * P].bitcast(FP8X4),
                lhsT_scale=scales[:, t * P : (t + 1) * P],
                rhs=upd_codes.bitcast(FP8X4),
                rhs_scale=upd_scales,
                start=(i == 0),
                stop=(i == len(passes) - 1),
            )

        for c in range(AHEAD):
            load_for_chunk(c)

        for i in range(len(passes)):
            slices = prepare(i)
            if i >= 1:
                quantise(i - 1)
            quantise_slices(slices)
            if i >= LAG:
                for t in range(TILES):
                    multiply(i - LAG, t)
        quantise(len(passes) - 1)
        for t in range(TILES):
            for i in range(len(passes) - LAG, len(passes)):
                multiply(i, t)

        stats = const.tile([P, TILES, 6], F32)
        mean_var = const.tile([P, TILES, 2], F32)
        for t in range(TILES):
            nc.vector.bn_stats(out=stats[:, t, :], in_=acc[t][:])
            nc.vector.bn_aggr(out=mean_var[:, t, :], in_=stats[:, t, :])
        var_eps = const.tile([P, TILES], F32)
        nc.vector.tensor_scalar_add(out=var_eps[:], in0=mean_var[:, :, 1], scalar1=BN_EPS)
        std = const.tile([P, TILES], F32)
        nc.scalar.sqrt(out=std[:], in_=var_eps[:])
        inv_std = const.tile([P, TILES], F32)
        nc.vector.reciprocal(out=inv_std[:], in_=std[:])
        gain = const.tile([P, TILES], F32)
        nc.vector.tensor_tensor(out=gain[:], in0=gamma_beta[:, 0:TILES], in1=inv_std[:], op=ALU.mult)
        mean_gain = const.tile([P, TILES], F32)
        nc.vector.tensor_tensor(out=mean_gain[:], in0=mean_var[:, :, 0], in1=gain[:], op=ALU.mult)
        shift = const.tile([P, TILES], F32)
        nc.vector.tensor_tensor(out=shift[:], in0=gamma_beta[:, TILES : 2 * TILES], in1=mean_gain[:], op=ALU.subtract)
        out_tiles = out.rearrange("b (t p) h w -> t p b (h w)", p=P)
        for t in range(TILES):
            result = scratch.tile([P, BATCH, PIXELS], F32, tag="result")
            nc.scalar.activation(
                out=result[:].rearrange("p b n -> p (b n)"),
                in_=acc[t][:],
                func=ACT.Relu,
                scale=gain[:, t : t + 1],
                bias=shift[:, t : t + 1],
            )
            nc.sync.dma_start(out=out_tiles[t], in_=result[:])
